import numpy as np
import ml_dtypes


def mxq(x, axis, fmt="e4m3"):
    dtype, down = {"e4m3": (ml_dtypes.float8_e4m3fn, 7), "e5m2": (ml_dtypes.float8_e5m2, 14)}[fmt]
    v = np.moveaxis(np.asarray(x, np.float32).astype(ml_dtypes.bfloat16).astype(np.float64), axis, -1)
    blocks = v.reshape(v.shape[:-1] + (-1, 32))
    amax = np.abs(blocks).max(-1, keepdims=True)
    byte = np.maximum(np.where(amax > 0, np.frexp(amax)[1] - 1 + 127, 0) - down, 1)
    scale = np.exp2(byte - 127.0)
    codes = (blocks / scale).astype(np.float32).astype(dtype).astype(np.float64)
    return np.moveaxis((codes * scale).reshape(v.shape), -1, axis)


WIDE = False


def mx_kscale(k):
    if not WIDE:
        return np.ones(k)
    levels = np.array([10, -10, 5, -5, 0])
    a = np.random.permutation(np.resize(levels, k // 512 * 4)).reshape(k // 512, 4)
    idx = np.arange(k)
    return np.exp2(a[idx // 512, idx % 128 // 32])


BF16 = ml_dtypes.bfloat16


def bf(x):
    return np.asarray(x, np.float32).astype(BF16)


def f64(x):
    return np.asarray(x).astype(np.float64)


B, S, D, H, DN, DR, DV, RQ, RKV = 2, 256, 2048, 16, 64, 128, 128, 1536, 512
THETA = 10000.0
EPS = 1e-6


def rmsnorm(v, w):
    return v * (1.0 / np.sqrt(np.mean(v * v, axis=-1, keepdims=True) + EPS)) * w


def rotate_half(v):
    v1 = v[..., ::2]
    v2 = v[..., 1::2]
    return np.stack((-v2, v1), axis=-1).reshape(v.shape)


def rope_cache():
    inv_freq = 1.0 / THETA ** (np.arange(0, DR, 2) / DR)
    freqs = np.outer(np.arange(S), inv_freq)
    emb = np.concatenate((freqs, freqs), -1)
    return np.cos(emb), np.sin(emb)


def apply_rope(v, cos, sin):
    return v * cos[None, None] + rotate_half(v) * sin[None, None]


def setup_inputs():
    s, t = mx_kscale(D), mx_kscale(RKV)
    return {"x": bf(np.random.standard_normal((B, S, D)) * s),
            "Wkva": bf(np.random.standard_normal((D, RKV + DR)) / np.sqrt(D) / s[:, None]),
            "kv_a_norm_w": bf((1.0 + 0.1 * np.random.standard_normal(RKV)) * t),
            "Wkvb": bf(np.random.standard_normal((RKV, H * (DN + DV))) / np.sqrt(RKV) / t[:, None])}


def reference(x, Wkva, kv_a_norm_w, Wkvb):
    kv_a = mxq(f64(x), 2, "e4m3") @ mxq(f64(Wkva), 0, "e4m3")
    kv_latent, k_rope_shared = kv_a[..., :RKV], kv_a[..., RKV:]
    h = rmsnorm(kv_latent, f64(kv_a_norm_w))
    kv = mxq(h, 2, "e4m3") @ mxq(f64(Wkvb), 0, "e4m3")
    kv = kv.reshape(B, S, H, DN + DV).transpose(0, 2, 1, 3)
    k_nope, v = kv[..., :DN], kv[..., DN:]
    cos, sin = rope_cache()
    k_rope = apply_rope(k_rope_shared[:, None], cos, sin)
    k_rope = np.broadcast_to(k_rope, (B, H, S, DR))
    k_final = np.concatenate([k_nope, k_rope], -1)
    return k_final, v

@@ -1,0 +1,282 @@
+import math
+from contextlib import ExitStack
+
+import concourse.mybir as mybir
+from concourse.masks import make_identity
+
+F32 = mybir.dt.float32
+BF16 = mybir.dt.bfloat16
+I32 = mybir.dt.int32
+U32 = mybir.dt.uint32
+U8 = mybir.dt.uint8
+FP8X4 = mybir.dt.float8_e4m3fn_x4
+ALU = mybir.AluOpType
+ACT = mybir.ActivationFunctionType
+
+P = 128
+PACK = 4
+K_PASS = P * PACK
+
+BATCH, SEQ, D_MODEL = 2, 256, 2048
+HEADS, D_NOPE, D_ROPE, D_V = 16, 64, 128, 128
+LATENT = 512
+A_COLS = LATENT + D_ROPE
+HEAD_COLS = D_NOPE + D_V
+THETA = 10000.0
+EPS = 1e-6
+
+A_PASSES = D_MODEL // K_PASS
+ROWS = SEQ // P
+GROUP_HEADS = 4
+GROUPS = HEADS // GROUP_HEADS
+GROUP_COLS = GROUP_HEADS * HEAD_COLS
+V_COLS = GROUP_HEADS * D_V
+NOPE_COLS = GROUP_HEADS * D_NOPE
+
+ROUND_MAGIC = 1.5 * 2.0**23
+COS, SIN = 0, 1
+
+FLOPS = 2 * BATCH * SEQ * (D_MODEL * A_COLS + LATENT * HEADS * HEAD_COLS)
+
+
+def tile_multiheadlatentattention_pb_kernel(tc, x, Wkva, kv_a_norm_w, Wkvb, out_0, out_1):
+    nc = tc.nc
+    with ExitStack() as ctx:
+        const = ctx.enter_context(tc.tile_pool(name="const", bufs=1))
+        raw = ctx.enter_context(tc.tile_pool(name="raw", bufs=1))
+        keep = ctx.enter_context(tc.tile_pool(name="keep", bufs=1))
+        stage = ctx.enter_context(tc.tile_pool(name="stage", bufs=2))
+        outp = ctx.enter_context(tc.tile_pool(name="outp", bufs=3))
+        psum = ctx.enter_context(tc.psum_pool(name="psum", bufs=8))
+
+        wa_raw = []
+        for c in range(A_PASSES):
+            t = raw.tile([P, PACK, A_COLS], BF16, name="wa_raw%d" % c)
+            nc.sync.dma_start(
+                out=t[:].rearrange("q (u e) n -> q u (e n)", u=2),
+                in_=Wkva[c * K_PASS : (c + 1) * K_PASS, :].rearrange("(u q e) n -> q u (e n)", u=2, e=2),
+            )
+            wa_raw.append(t)
+        x_raw = {}
+        for b in range(BATCH):
+            for j in range(ROWS):
+                t = raw.tile([P, D_MODEL], BF16, name="x_raw%d%d" % (b, j))
+                nc.sync.dma_start(out=t[:], in_=x[b].rearrange("(p j) d -> p j d", j=ROWS)[:, j, :])
+                x_raw[(b, j)] = t
+        wb_raw = []
+        for g in range(GROUPS):
+            t = raw.tile([P, PACK, GROUP_COLS], BF16, name="wb_raw%d" % g)
+            nc.sync.dma_start(
+                out=t[:],
+                in_=Wkvb[:, g * GROUP_COLS : (g + 1) * GROUP_COLS].rearrange("(t p) n -> p t n", p=P),
+            )
+            wb_raw.append(t)
+
+        ident_f32 = const.tile([P, P], F32)
+        make_identity(nc, ident_f32[:])
+        ident_bf = const.tile([P, P], BF16)
+        make_identity(nc, ident_bf[:])
+
+        gain_row = const.tile([P, LATENT], BF16)
+        nc.vector.memset(gain_row[:], 0.0)
+        nc.scalar.dma_start(out=gain_row[0:1, :], in_=kv_a_norm_w.rearrange("(o n) -> o n", o=1))
+        ones = const.tile([P, P], BF16)
+        nc.vector.memset(ones[:], 1.0)
+        gain_ps = psum.tile([P, LATENT], F32, tag="bank")
+        nc.tensor.matmul(out=gain_ps[:], lhsT=ones[:], rhs=gain_row[:], start=True, stop=True)
+        gain = const.tile([P, LATENT], F32)
+        nc.scalar.copy(out=gain[:], in_=gain_ps[:])
+
+        eps_col = const.tile([P, 1], F32)
+        nc.vector.memset(eps_col[:], EPS)
+
+        turns_per_pos = const.tile([P, D_ROPE], F32)
+        nc.vector.memset(turns_per_pos[:], 1.0)
+        nc.vector.tensor_scalar_mul(out=turns_per_pos[:], in0=turns_per_pos[:], scalar1=1.0 / (2.0 * math.pi))
+        for level in range(6):
+            bit = 2**level
+            has_bit = turns_per_pos[:].rearrange("p (a two c) -> p a two c", two=2, c=bit)[:, :, 1, :]
+            nc.vector.tensor_scalar_mul(out=has_bit, in0=has_bit, scalar1=THETA ** (-bit / 64.0))
+        pos_int = const.tile([P, ROWS], I32)
+        nc.gpsimd.iota(pos_int[:], pattern=[[1, ROWS]], base=0, channel_multiplier=ROWS)
+        pos = const.tile([P, ROWS], F32)
+        nc.vector.tensor_copy(out=pos[:], in_=pos_int[:])
+        turns = const.tile([P, 2, ROWS, D_ROPE], F32)
+        for j in range(ROWS):
+            nc.vector.tensor_scalar(
+                out=turns[:, COS, j, :], in0=turns_per_pos[:], scalar1=pos[:, j : j + 1], scalar2=0.25,
+                op0=ALU.mult, op1=ALU.add,
+            )
+            nc.vector.tensor_scalar(
+                out=turns[:, SIN, j, :], in0=turns_per_pos[:], scalar1=pos[:, j : j + 1], scalar2=None,
+                op0=ALU.mult,
+            )
+        whole = const.tile([P, 2, ROWS, D_ROPE], F32)
+        nc.vector.tensor_scalar(
+            out=whole[:], in0=turns[:], scalar1=ROUND_MAGIC, scalar2=ROUND_MAGIC, op0=ALU.add, op1=ALU.subtract
+        )
+        part = const.tile([P, 2, ROWS, D_ROPE], F32)
+        nc.vector.tensor_tensor(out=part[:], in0=turns[:], in1=whole[:], op=ALU.subtract)
+        table = const.tile([P, 2, ROWS, D_ROPE], F32)
+        nc.scalar.activation(out=table[:], in_=part[:], func=ACT.Sin, scale=2.0 * math.pi)
+        sin_even = table[:, SIN, :, :].rearrange("p j (m e) -> p (j m) e", e=2)[:, :, 0]
+        nc.vector.tensor_scalar_mul(out=sin_even, in0=sin_even, scalar1=-1.0)
+        warm = const.tile([P, 1], F32)
+        nc.scalar.activation(out=warm[:], in_=table[:, COS, 0, 0:1], func=ACT.Sqrt, scale=0.0, bias=eps_col[:, 0:1])
+
+        wa_codes = keep.tile([P, A_PASSES, A_COLS], U32, align_bytes=64)
+        wa_scales = keep.tile([P, A_PASSES, A_COLS], U8, align_bytes=64)
+        x_codes = keep.tile([P, BATCH, ROWS, A_PASSES * P], U32, align_bytes=64)
+        x_scales = keep.tile([P, BATCH, ROWS, A_PASSES * P], U8, align_bytes=64)
+        h_codes = keep.tile([P, BATCH, ROWS * P], U32, align_bytes=64)
+        h_scales = keep.tile([P, BATCH, ROWS * P], U8, align_bytes=64)
+        wv_codes = keep.tile([P, GROUPS, V_COLS], U32, align_bytes=64)
+        wv_scales = keep.tile([P, GROUPS, V_COLS], U8, align_bytes=64)
+        wn_codes = keep.tile([P, GROUPS, NOPE_COLS], U32, align_bytes=64)
+        wn_scales = keep.tile([P, GROUPS, NOPE_COLS], U8, align_bytes=64)
+
+        def quantise(codes, scales, grouped):
+            nc.vector.quantize_mx(out=codes.bitcast(FP8X4), scales=scales, in_=grouped)
+
+        HALF_COLS = A_COLS // 2
+        for c in range(A_PASSES):
+            wa_grouped = stage.tile([P, A_COLS, PACK], BF16, align_bytes=64)
+            nc.vector.tensor_copy(
+                out=wa_grouped[:, 0:HALF_COLS, :].rearrange("p (c i) t -> p c t i", i=4),
+                in_=wa_raw[c][:, :, 0:HALF_COLS].rearrange("p t (c i) -> p c t i", i=4),
+            )
+            nc.scalar.copy(
+                out=wa_grouped[:, HALF_COLS:A_COLS, :].rearrange("p (c i) t -> p c t i", i=4),
+                in_=wa_raw[c][:, :, HALF_COLS:A_COLS].rearrange("p t (c i) -> p c t i", i=4),
+            )
+            for cols in (slice(0, LATENT), slice(LATENT, A_COLS)):
+                quantise(
+                    wa_codes[:, c, cols], wa_scales[:, c, cols],
+                    wa_grouped[:, cols, :].rearrange("p n t -> p (n t)"),
+                )
+
+        rope_out = {}
+        for b in range(BATCH):
+            r_ps = psum.tile([P, ROWS, D_ROPE], F32, tag="bank")
+            c_ps = []
+            for j in range(ROWS):
+                x_words = x_raw[(b, j)][:].bitcast(F32)
+                x_grouped = stage.tile([P, A_PASSES * P * PACK], BF16, align_bytes=64)
+                xg_words = x_grouped[:].bitcast(F32).rearrange("p (c r u) -> p c r u", c=A_PASSES, u=2)
+                for half in range(2):
+                    xT = psum.tile([P, 2, 2, P], F32, tag="bank")
+                    for c2 in range(2):
+                        for u in range(2):
+                            w0 = ((2 * half + c2) * 2 + u) * P
+                            nc.tensor.transpose(xT[:, c2, u, :], x_words[:, w0 : w0 + P], ident_f32[:])
+                    nc.scalar.copy(
+                        out=xg_words[:, 2 * half : 2 * half + 2, :, :],
+                        in_=xT[:].rearrange("p c u r -> p c r u"),
+                    )
+                quantise(x_codes[:, b, j, :], x_scales[:, b, j, :], x_grouped[:])
+
+                acc = psum.tile([P, LATENT], F32, tag="bank")
+                for out_ap, cols in ((acc[:], slice(0, LATENT)), (r_ps[:, j, :], slice(LATENT, A_COLS))):
+                    for c in range(A_PASSES):
+                        toks = slice(c * P, (c + 1) * P)
+                        nc.tensor.matmul_mx(
+                            out=out_ap,
+                            lhsT=x_codes[:, b, j, toks].bitcast(FP8X4),
+                            lhsT_scale=x_scales[:, b, j, toks],
+                            rhs=wa_codes[:, c, cols].bitcast(FP8X4),
+                            rhs_scale=wa_scales[:, c, cols],
+                            start=(c == 0),
+                            stop=(c == A_PASSES - 1),
+                        )
+                c_ps.append(acc)
+
+            sumsq = stage.tile([P, ROWS], F32)
+            for j in range(ROWS):
+                squares = stage.tile([P, LATENT], BF16)
+                nc.scalar.activation(out=squares[:], in_=c_ps[j][:], func=ACT.Square, accum_out=sumsq[:, j : j + 1])
+            rms = stage.tile([P, ROWS], F32)
+            nc.scalar.activation(out=rms[:], in_=sumsq[:], func=ACT.Sqrt, scale=1.0 / LATENT, bias=eps_col[:, 0:1])
+            rstd = stage.tile([P, ROWS], F32)
+            nc.vector.reciprocal(out=rstd[:], in_=rms[:])
+            hT = psum.tile([P, ROWS, PACK, P], BF16, tag="bank")
+            for j in range(ROWS):
+                h = stage.tile([P, LATENT], BF16)
+                nc.vector.scalar_tensor_tensor(
+                    out=h[:], in0=c_ps[j][:], scalar=rstd[:, j : j + 1], in1=gain[:], op0=ALU.mult, op1=ALU.mult
+                )
+                for t in range(PACK):
+                    nc.tensor.transpose(hT[:, j, t, :], h[:, t * P : (t + 1) * P], ident_bf[:])
+            h_grouped = stage.tile([P, ROWS * P * PACK], BF16, align_bytes=64)
+            nc.vector.tensor_copy(
+                out=h_grouped[:].rearrange("p (j r t) -> p j r t", j=ROWS, t=PACK),
+                in_=hT[:].rearrange("p j t r -> p j r t"),
+            )
+            quantise(h_codes[:, b, :], h_scales[:, b, :], h_grouped[:])
+
+            by_cos = stage.tile([P, ROWS, D_ROPE], F32)
+            nc.vector.tensor_tensor(out=by_cos[:], in0=r_ps[:], in1=table[:, COS, :, :], op=ALU.mult)
+            by_sin = stage.tile([P, ROWS, D_ROPE], F32)
+            r_pairs = r_ps[:].rearrange("p j (m e) -> p (j m) e", e=2)
+            sin_pairs = table[:, SIN, :, :].rearrange("p j (m e) -> p (j m) e", e=2)
+            out_pairs = by_sin[:].rearrange("p j (m e) -> p (j m) e", e=2)
+            for e in range(2):
+                nc.vector.tensor_tensor(
+                    out=out_pairs[:, :, e], in0=r_pairs[:, :, 1 - e], in1=sin_pairs[:, :, e], op=ALU.mult
+                )
+            rotated = keep.tile([P, ROWS, D_ROPE], F32, name="rotated%d" % b)
+            nc.vector.tensor_tensor(out=rotated[:], in0=by_cos[:], in1=by_sin[:], op=ALU.add)
+            rope_out[b] = rotated
+
+        for g in range(GROUPS):
+            by_head = wb_raw[g][:].rearrange("p t (h f) -> p h f t", f=HEAD_COLS)
+            wv_grouped = stage.tile([P, V_COLS * PACK], BF16, align_bytes=64)
+            nc.vector.tensor_copy(
+                out=wv_grouped[:].rearrange("p (h f t) -> p h f t", h=GROUP_HEADS, t=PACK),
+                in_=by_head[:, :, D_NOPE:HEAD_COLS, :],
+            )
+            wn_grouped = stage.tile([P, NOPE_COLS * PACK], BF16, align_bytes=64)
+            nc.scalar.copy(
+                out=wn_grouped[:].rearrange("p (h f t) -> p h f t", h=GROUP_HEADS, t=PACK),
+                in_=by_head[:, :, 0:D_NOPE, :],
+            )
+            quantise(wv_codes[:, g, :], wv_scales[:, g, :], wv_grouped[:])
+            quantise(wn_codes[:, g, :], wn_scales[:, g, :], wn_grouped[:])
+
+            heads = slice(g * GROUP_HEADS, (g + 1) * GROUP_HEADS)
+            for b in range(BATCH):
+                v_tile = outp.tile([P, GROUP_HEADS, ROWS, D_V], F32)
+                k_tile = outp.tile([P, GROUP_HEADS, ROWS, D_NOPE + D_ROPE], F32)
+                nope_ps = psum.tile([P, ROWS, NOPE_COLS], F32, tag="bank")
+                for j in range(ROWS):
+                    toks = slice(j * P, (j + 1) * P)
+                    v_ps = psum.tile([P, V_COLS], F32, tag="bank")
+                    for out_ap, codes, scales in (
+                        (v_ps[:], wv_codes, wv_scales),
+                        (nope_ps[:, j, :], wn_codes, wn_scales),
+                    ):
+                        nc.tensor.matmul_mx(
+                            out=out_ap,
+                            lhsT=h_codes[:, b, toks].bitcast(FP8X4),
+                            lhsT_scale=h_scales[:, b, toks],
+                            rhs=codes[:, g, :].bitcast(FP8X4),
+                            rhs_scale=scales[:, g, :],
+                            start=True,
+                            stop=True,
+                        )
+                    nc.scalar.copy(out=v_tile[:, :, j, :], in_=v_ps[:].rearrange("p (h f) -> p h f", h=GROUP_HEADS))
+                nc.sync.dma_start(
+                    out=out_1[b, heads].rearrange("h (p j) f -> p h (j f)", j=ROWS),
+                    in_=v_tile[:].rearrange("p h j f -> p h (j f)"),
+                )
+                nc.vector.tensor_copy(
+                    out=k_tile[:, :, :, 0:D_NOPE],
+                    in_=nope_ps[:].rearrange("p j (h f) -> p h j f", h=GROUP_HEADS),
+                )
+                nc.vector.tensor_copy(
+                    out=k_tile[:, :, :, D_NOPE:],
+                    in_=rope_out[b][:].unsqueeze(1).to_broadcast([P, GROUP_HEADS, ROWS, D_ROPE]),
+                )
+                nc.sync.dma_start(
+                    out=out_0[b, heads].rearrange("h (p j) f -> p h (j f)", j=ROWS),
+                    in_=k_tile[:].rearrange("p h j f -> p h (j f)"),
+                )

@@ -27,11 +27,14 @@ EPS = 1e-6
 
 A_PASSES = D_MODEL // K_PASS
 ROWS = SEQ // P
+TILES = BATCH * ROWS
 GROUP_HEADS = 4
 GROUPS = HEADS // GROUP_HEADS
 GROUP_COLS = GROUP_HEADS * HEAD_COLS
 V_COLS = GROUP_HEADS * D_V
 NOPE_COLS = GROUP_HEADS * D_NOPE
+K_BUFFERS = 2
+RUN = 4
 
 ROUND_MAGIC = 1.5 * 2.0**23
 COS, SIN = 0, 1
@@ -46,69 +49,85 @@ def tile_multiheadlatentattention_pb_kernel(tc, x, Wkva, kv_a_norm_w, Wkvb, out_
         raw = ctx.enter_context(tc.tile_pool(name="raw", bufs=1))
         keep = ctx.enter_context(tc.tile_pool(name="keep", bufs=1))
         stage = ctx.enter_context(tc.tile_pool(name="stage", bufs=2))
-        outp = ctx.enter_context(tc.tile_pool(name="outp", bufs=3))
+        per_tile = ctx.enter_context(tc.tile_pool(name="per_tile", bufs=TILES))
         psum = ctx.enter_context(tc.psum_pool(name="psum", bufs=8))
+        ctx.enter_context(tc.manual_schedule())
 
-        wa_raw = []
-        for c in range(A_PASSES):
-            t = raw.tile([P, PACK, A_COLS], BF16, name="wa_raw%d" % c)
-            nc.sync.dma_start(
-                out=t[:].rearrange("q (u e) n -> q u (e n)", u=2),
-                in_=Wkva[c * K_PASS : (c + 1) * K_PASS, :].rearrange("(u q e) n -> q u (e n)", u=2, e=2),
+        def quantise(codes, scales, grouped):
+            nc.vector.quantize_mx(out=codes.bitcast(FP8X4), scales=scales, in_=grouped)
+
+        def mx_pass(out, lhs_codes, lhs_scales, rhs_codes, rhs_scales, start, stop):
+            nc.tensor.matmul_mx(
+                out=out,
+                lhsT=lhs_codes.bitcast(FP8X4),
+                lhsT_scale=lhs_scales,
+                rhs=rhs_codes.bitcast(FP8X4),
+                rhs_scale=rhs_scales,
+                start=start,
+                stop=stop,
             )
-            wa_raw.append(t)
-        x_raw = {}
+
+        gain_row = const.tile([P, LATENT], BF16)
+        nc.vector.memset(gain_row[:], 0.0)
+        nc.sync.dma_start(out=gain_row[0:1, :], in_=kv_a_norm_w.rearrange("(o n) -> o n", o=1))
+        x_raw = []
         for b in range(BATCH):
             for j in range(ROWS):
-                t = raw.tile([P, D_MODEL], BF16, name="x_raw%d%d" % (b, j))
-                nc.sync.dma_start(out=t[:], in_=x[b].rearrange("(p j) d -> p j d", j=ROWS)[:, j, :])
-                x_raw[(b, j)] = t
+                x_tile = raw.tile([P, D_MODEL], BF16, name="x_raw%d%d" % (b, j))
+                nc.sync.dma_start(out=x_tile[:], in_=x[b].rearrange("(p j) d -> p j d", j=ROWS)[:, j, :])
+                x_raw.append(x_tile)
+        wa_raw = []
+        for c in range(A_PASSES):
+            wa_tile = raw.tile([P, PACK, A_COLS], BF16, name="wa_raw%d" % c)
+            nc.sync.dma_start(
+                out=wa_tile[:].rearrange("q (u e) n -> q u (e n)", u=2),
+                in_=Wkva[c * K_PASS : (c + 1) * K_PASS, :].rearrange("(u q e) n -> q u (e n)", u=2, e=2),
+            )
+            wa_raw.append(wa_tile)
         wb_raw = []
         for g in range(GROUPS):
-            t = raw.tile([P, PACK, GROUP_COLS], BF16, name="wb_raw%d" % g)
+            wb_tile = raw.tile([P, PACK, GROUP_COLS], BF16, name="wb_raw%d" % g)
             nc.sync.dma_start(
-                out=t[:],
+                out=wb_tile[:],
                 in_=Wkvb[:, g * GROUP_COLS : (g + 1) * GROUP_COLS].rearrange("(t p) n -> p t n", p=P),
             )
-            wb_raw.append(t)
+            wb_raw.append(wb_tile)
 
         ident_f32 = const.tile([P, P], F32)
         make_identity(nc, ident_f32[:])
         ident_bf = const.tile([P, P], BF16)
         make_identity(nc, ident_bf[:])
-
-        gain_row = const.tile([P, LATENT], BF16)
-        nc.vector.memset(gain_row[:], 0.0)
-        nc.scalar.dma_start(out=gain_row[0:1, :], in_=kv_a_norm_w.rearrange("(o n) -> o n", o=1))
-        ones = const.tile([P, P], BF16)
-        nc.vector.memset(ones[:], 1.0)
-        gain_ps = psum.tile([P, LATENT], F32, tag="bank")
-        nc.tensor.matmul(out=gain_ps[:], lhsT=ones[:], rhs=gain_row[:], start=True, stop=True)
-        gain = const.tile([P, LATENT], F32)
-        nc.scalar.copy(out=gain[:], in_=gain_ps[:])
-
-        eps_col = const.tile([P, 1], F32)
-        nc.vector.memset(eps_col[:], EPS)
-
-        turns_per_pos = const.tile([P, D_ROPE], F32)
-        nc.vector.memset(turns_per_pos[:], 1.0)
-        nc.vector.tensor_scalar_mul(out=turns_per_pos[:], in0=turns_per_pos[:], scalar1=1.0 / (2.0 * math.pi))
-        for level in range(6):
-            bit = 2**level
-            has_bit = turns_per_pos[:].rearrange("p (a two c) -> p a two c", two=2, c=bit)[:, :, 1, :]
-            nc.vector.tensor_scalar_mul(out=has_bit, in0=has_bit, scalar1=THETA ** (-bit / 64.0))
         pos_int = const.tile([P, ROWS], I32)
         nc.gpsimd.iota(pos_int[:], pattern=[[1, ROWS]], base=0, channel_multiplier=ROWS)
+        minus_half = const.tile([P, 1], F32)
+        nc.gpsimd.memset(minus_half[:], -0.5)
+        zero_col = const.tile([P, 1], F32)
+        nc.gpsimd.memset(zero_col[:], 0.0)
+
+        warm = const.tile([P, 1], F32)
+        nc.scalar.activation(out=warm[:], in_=zero_col[:], func=ACT.Sin)
+
+        ones = const.tile([P, P], BF16)
+        nc.vector.memset(ones[:], 1.0)
+
+        per_pos = const.tile([P, D_ROPE], F32)
+        nc.vector.memset(per_pos[:], 1.0)
+        for level in range(6):
+            bit = 2**level
+            has_bit = per_pos[:].rearrange("p (a two c) -> p a two c", two=2, c=bit)[:, :, 1, :]
+            nc.vector.tensor_scalar_mul(out=has_bit, in0=has_bit, scalar1=THETA ** (-bit / 64.0))
         pos = const.tile([P, ROWS], F32)
         nc.vector.tensor_copy(out=pos[:], in_=pos_int[:])
+        pos_turns = const.tile([P, ROWS], F32)
+        nc.vector.tensor_scalar_mul(out=pos_turns[:], in0=pos[:], scalar1=1.0 / (2.0 * math.pi))
         turns = const.tile([P, 2, ROWS, D_ROPE], F32)
         for j in range(ROWS):
             nc.vector.tensor_scalar(
-                out=turns[:, COS, j, :], in0=turns_per_pos[:], scalar1=pos[:, j : j + 1], scalar2=0.25,
+                out=turns[:, COS, j, :], in0=per_pos[:], scalar1=pos_turns[:, j : j + 1], scalar2=0.25,
                 op0=ALU.mult, op1=ALU.add,
             )
             nc.vector.tensor_scalar(
-                out=turns[:, SIN, j, :], in0=turns_per_pos[:], scalar1=pos[:, j : j + 1], scalar2=None,
+                out=turns[:, SIN, j, :], in0=per_pos[:], scalar1=pos_turns[:, j : j + 1], scalar2=None,
                 op0=ALU.mult,
             )
         whole = const.tile([P, 2, ROWS, D_ROPE], F32)
@@ -117,106 +136,163 @@ def tile_multiheadlatentattention_pb_kernel(tc, x, Wkva, kv_a_norm_w, Wkvb, out_
         )
         part = const.tile([P, 2, ROWS, D_ROPE], F32)
         nc.vector.tensor_tensor(out=part[:], in0=turns[:], in1=whole[:], op=ALU.subtract)
-        table = const.tile([P, 2, ROWS, D_ROPE], F32)
-        nc.scalar.activation(out=table[:], in_=part[:], func=ACT.Sin, scale=2.0 * math.pi)
-        sin_even = table[:, SIN, :, :].rearrange("p j (m e) -> p (j m) e", e=2)[:, :, 0]
+        sin_even = part[:, SIN, :, :].rearrange("p j (m e) -> p (j m) e", e=2)[:, :, 0]
         nc.vector.tensor_scalar_mul(out=sin_even, in0=sin_even, scalar1=-1.0)
-        warm = const.tile([P, 1], F32)
-        nc.scalar.activation(out=warm[:], in_=table[:, COS, 0, 0:1], func=ACT.Sqrt, scale=0.0, bias=eps_col[:, 0:1])
+        table = const.tile([P, 2, ROWS, D_ROPE], F32)
 
+        x_codes = keep.tile([P, TILES, A_PASSES * P], U32, align_bytes=64)
+        x_scales = keep.tile([P, TILES, A_PASSES * P], U8, align_bytes=64)
         wa_codes = keep.tile([P, A_PASSES, A_COLS], U32, align_bytes=64)
         wa_scales = keep.tile([P, A_PASSES, A_COLS], U8, align_bytes=64)
-        x_codes = keep.tile([P, BATCH, ROWS, A_PASSES * P], U32, align_bytes=64)
-        x_scales = keep.tile([P, BATCH, ROWS, A_PASSES * P], U8, align_bytes=64)
-        h_codes = keep.tile([P, BATCH, ROWS * P], U32, align_bytes=64)
-        h_scales = keep.tile([P, BATCH, ROWS * P], U8, align_bytes=64)
+        h_codes = keep.tile([P, TILES * P], U32, align_bytes=64)
+        h_scales = keep.tile([P, TILES * P], U8, align_bytes=64)
         wv_codes = keep.tile([P, GROUPS, V_COLS], U32, align_bytes=64)
         wv_scales = keep.tile([P, GROUPS, V_COLS], U8, align_bytes=64)
         wn_codes = keep.tile([P, GROUPS, NOPE_COLS], U32, align_bytes=64)
         wn_scales = keep.tile([P, GROUPS, NOPE_COLS], U8, align_bytes=64)
 
-        def quantise(codes, scales, grouped):
-            nc.vector.quantize_mx(out=codes.bitcast(FP8X4), scales=scales, in_=grouped)
+        for i in range(TILES):
+            x_words = x_raw[i][:].bitcast(F32)
+            x_grouped = per_tile.tile([P, A_PASSES * P * PACK], BF16, align_bytes=64)
+            xg_words = x_grouped[:].bitcast(F32).rearrange("p (c r u) -> p c r u", c=A_PASSES, u=2)
+            for half in range(2):
+                xT = psum.tile([P, 2, 2, P], F32, tag="bank")
+                for c2 in range(2):
+                    for u in range(2):
+                        w0 = ((2 * half + c2) * 2 + u) * P
+                        nc.tensor.transpose(xT[:, c2, u, :], x_words[:, w0 : w0 + P], ident_f32[:])
+                nc.scalar.copy(
+                    out=xg_words[:, 2 * half : 2 * half + 2, :, :],
+                    in_=xT[:].rearrange("p c u r -> p c r u"),
+                )
+            quantise(x_codes[:, i, :], x_scales[:, i, :], x_grouped[:])
+
+        gain_ps = psum.tile([P, LATENT], F32, tag="bank")
+        nc.tensor.matmul(out=gain_ps[:], lhsT=ones[:], rhs=gain_row[:], start=True, stop=True)
+        gain = const.tile([P, LATENT], F32)
+        nc.vector.tensor_copy(out=gain[:], in_=gain_ps[:])
 
         HALF_COLS = A_COLS // 2
+        latent_ps = []
+        for i in range(TILES):
+            latent_ps.append(psum.tile([P, LATENT], F32, tag="bank", name="latent_ps%d" % i))
+        wa_grouped = []
         for c in range(A_PASSES):
-            wa_grouped = stage.tile([P, A_COLS, PACK], BF16, align_bytes=64)
+            grouped = per_tile.tile([P, A_COLS, PACK], BF16, align_bytes=64, name="wa_grouped%d" % c, tag="wa_grouped")
             nc.vector.tensor_copy(
-                out=wa_grouped[:, 0:HALF_COLS, :].rearrange("p (c i) t -> p c t i", i=4),
-                in_=wa_raw[c][:, :, 0:HALF_COLS].rearrange("p t (c i) -> p c t i", i=4),
+                out=grouped[:, 0:HALF_COLS, :].rearrange("p (c i) t -> p c t i", i=RUN),
+                in_=wa_raw[c][:, :, 0:HALF_COLS].rearrange("p t (c i) -> p c t i", i=RUN),
             )
             nc.scalar.copy(
-                out=wa_grouped[:, HALF_COLS:A_COLS, :].rearrange("p (c i) t -> p c t i", i=4),
-                in_=wa_raw[c][:, :, HALF_COLS:A_COLS].rearrange("p t (c i) -> p c t i", i=4),
+                out=grouped[:, HALF_COLS:A_COLS, :].rearrange("p (c i) t -> p c t i", i=RUN),
+                in_=wa_raw[c][:, :, HALF_COLS:A_COLS].rearrange("p t (c i) -> p c t i", i=RUN),
             )
-            for cols in (slice(0, LATENT), slice(LATENT, A_COLS)):
-                quantise(
-                    wa_codes[:, c, cols], wa_scales[:, c, cols],
-                    wa_grouped[:, cols, :].rearrange("p n t -> p (n t)"),
+            wa_grouped.append(grouped)
+            quantise(
+                wa_codes[:, c, 0:LATENT], wa_scales[:, c, 0:LATENT],
+                grouped[:, 0:LATENT, :].rearrange("p n t -> p (n t)"),
+            )
+            toks = slice(c * P, (c + 1) * P)
+            for i in range(TILES):
+                mx_pass(
+                    latent_ps[i][:], x_codes[:, i, toks], x_scales[:, i, toks],
+                    wa_codes[:, c, 0:LATENT], wa_scales[:, c, 0:LATENT],
+                    start=(c == 0), stop=(c == A_PASSES - 1),
                 )
 
-        rope_out = {}
-        for b in range(BATCH):
-            r_ps = psum.tile([P, ROWS, D_ROPE], F32, tag="bank")
-            c_ps = []
-            for j in range(ROWS):
-                x_words = x_raw[(b, j)][:].bitcast(F32)
-                x_grouped = stage.tile([P, A_PASSES * P * PACK], BF16, align_bytes=64)
-                xg_words = x_grouped[:].bitcast(F32).rearrange("p (c r u) -> p c r u", c=A_PASSES, u=2)
-                for half in range(2):
-                    xT = psum.tile([P, 2, 2, P], F32, tag="bank")
-                    for c2 in range(2):
-                        for u in range(2):
-                            w0 = ((2 * half + c2) * 2 + u) * P
-                            nc.tensor.transpose(xT[:, c2, u, :], x_words[:, w0 : w0 + P], ident_f32[:])
-                    nc.scalar.copy(
-                        out=xg_words[:, 2 * half : 2 * half + 2, :, :],
-                        in_=xT[:].rearrange("p c u r -> p c r u"),
-                    )
-                quantise(x_codes[:, b, j, :], x_scales[:, b, j, :], x_grouped[:])
+        nc.scalar.activation(out=table[:], in_=part[:], func=ACT.Sin, scale=2.0 * math.pi)
 
-                acc = psum.tile([P, LATENT], F32, tag="bank")
-                for out_ap, cols in ((acc[:], slice(0, LATENT)), (r_ps[:, j, :], slice(LATENT, A_COLS))):
-                    for c in range(A_PASSES):
-                        toks = slice(c * P, (c + 1) * P)
-                        nc.tensor.matmul_mx(
-                            out=out_ap,
-                            lhsT=x_codes[:, b, j, toks].bitcast(FP8X4),
-                            lhsT_scale=x_scales[:, b, j, toks],
-                            rhs=wa_codes[:, c, cols].bitcast(FP8X4),
-                            rhs_scale=wa_scales[:, c, cols],
-                            start=(c == 0),
-                            stop=(c == A_PASSES - 1),
-                        )
-                c_ps.append(acc)
+        for c in range(A_PASSES):
+            quantise(
+                wa_codes[:, c, LATENT:A_COLS], wa_scales[:, c, LATENT:A_COLS],
+                wa_grouped[c][:, LATENT:A_COLS, :].rearrange("p n t -> p (n t)"),
+            )
 
-            sumsq = stage.tile([P, ROWS], F32)
-            for j in range(ROWS):
-                squares = stage.tile([P, LATENT], BF16)
-                nc.scalar.activation(out=squares[:], in_=c_ps[j][:], func=ACT.Square, accum_out=sumsq[:, j : j + 1])
-            rms = stage.tile([P, ROWS], F32)
-            nc.scalar.activation(out=rms[:], in_=sumsq[:], func=ACT.Sqrt, scale=1.0 / LATENT, bias=eps_col[:, 0:1])
-            rstd = stage.tile([P, ROWS], F32)
-            nc.vector.reciprocal(out=rstd[:], in_=rms[:])
-            hT = psum.tile([P, ROWS, PACK, P], BF16, tag="bank")
-            for j in range(ROWS):
-                h = stage.tile([P, LATENT], BF16)
-                nc.vector.scalar_tensor_tensor(
-                    out=h[:], in0=c_ps[j][:], scalar=rstd[:, j : j + 1], in1=gain[:], op0=ALU.mult, op1=ALU.mult
-                )
-                for t in range(PACK):
-                    nc.tensor.transpose(hT[:, j, t, :], h[:, t * P : (t + 1) * P], ident_bf[:])
-            h_grouped = stage.tile([P, ROWS * P * PACK], BF16, align_bytes=64)
+        def regroup_wb(g, first_col, cols_per_head, grouped):
+            by_head = wb_raw[g][:].rearrange("p t (h f) -> p h t f", f=HEAD_COLS)
             nc.vector.tensor_copy(
-                out=h_grouped[:].rearrange("p (j r t) -> p j r t", j=ROWS, t=PACK),
-                in_=hT[:].rearrange("p j t r -> p j r t"),
+                out=grouped[:].rearrange("p (h c i t) -> p h c t i", h=GROUP_HEADS, i=RUN, t=PACK),
+                in_=by_head[:, :, :, first_col : first_col + cols_per_head].rearrange(
+                    "p h t (c i) -> p h c t i", i=RUN
+                ),
             )
-            quantise(h_codes[:, b, :], h_scales[:, b, :], h_grouped[:])
 
+        def regroup_v(g):
+            wv_grouped = stage.tile([P, V_COLS * PACK], BF16, align_bytes=64)
+            regroup_wb(g, D_NOPE, D_V, wv_grouped)
+            return wv_grouped
+
+        def regroup_nope(g):
+            wn_grouped = stage.tile([P, NOPE_COLS * PACK], BF16, align_bytes=64)
+            regroup_wb(g, 0, D_NOPE, wn_grouped)
+            return wn_grouped
+
+        wv_grouped0 = regroup_v(0)
+        quantise(wv_codes[:, 0, :], wv_scales[:, 0, :], wv_grouped0[:])
+
+        rope_ps = psum.tile([P, TILES, D_ROPE], F32, tag="bank")
+        for i in range(TILES):
+            for c in range(A_PASSES):
+                toks = slice(c * P, (c + 1) * P)
+                mx_pass(
+                    rope_ps[:, i, :], x_codes[:, i, toks], x_scales[:, i, toks],
+                    wa_codes[:, c, LATENT:A_COLS], wa_scales[:, c, LATENT:A_COLS],
+                    start=(c == 0), stop=(c == A_PASSES - 1),
+                )
+
+        mean_sq = const.tile([P, TILES], F32)
+        mean_eps = const.tile([P, TILES], F32)
+        rstd = const.tile([P, TILES], F32)
+        for i in range(TILES):
+            col = slice(i, i + 1)
+            squares = stage.tile([P, LATENT], BF16)
+            nc.scalar.activation(
+                out=squares[:], in_=latent_ps[i][:], func=ACT.Square, scale=1.0 / math.sqrt(LATENT),
+                accum_out=mean_sq[:, col],
+            )
+            nc.gpsimd.tensor_scalar(
+                out=mean_eps[:, col], in0=mean_sq[:, col], scalar1=1.0, scalar2=EPS, op0=ALU.mult, op1=ALU.add
+            )
+            nc.gpsimd.tensor_tensor(out=rstd[:, col], in0=mean_eps[:, col], in1=minus_half[:], op=ALU.pow)
+        hT = []
+        for i in range(TILES):
+            h = per_tile.tile([P, LATENT], BF16)
+            nc.vector.scalar_tensor_tensor(
+                out=h[:], in0=latent_ps[i][:], scalar=rstd[:, i : i + 1], in1=gain[:], op0=ALU.mult, op1=ALU.mult
+            )
+            hT_ps = psum.tile([P, PACK, P], BF16, tag="bank", name="hT_ps%d" % i)
+            for t in range(PACK):
+                nc.tensor.transpose(hT_ps[:, t, :], h[:, t * P : (t + 1) * P], ident_bf[:])
+            hT.append(hT_ps)
+        h_grouped = keep.tile([P, TILES, P, PACK], BF16, align_bytes=64)
+        for i in range(TILES):
+            nc.scalar.copy(out=h_grouped[:, i, :, :], in_=hT[i][:].rearrange("p t r -> p r t"))
+
+        def quantise_h(b):
+            toks = slice(b * ROWS * P, (b + 1) * ROWS * P)
+            quantise(
+                h_codes[:, toks], h_scales[:, toks],
+                h_grouped[:, b * ROWS : (b + 1) * ROWS, :, :].rearrange("p i r t -> p (i r t)"),
+            )
+
+        quantise_h(0)
+        wn_grouped0 = regroup_nope(0)
+        quantise_h(1)
+        quantise(wn_codes[:, 0, :], wn_scales[:, 0, :], wn_grouped0[:])
+
+        k_tiles = {}
+        for slot in range(K_BUFFERS):
+            for b in range(BATCH):
+                k_tiles[(slot, b)] = keep.tile(
+                    [P, GROUP_HEADS, ROWS, D_NOPE + D_ROPE], F32, name="k_tile%d%d" % (slot, b)
+                )
+
+        def rotate(b):
+            r_ps = rope_ps[:, b * ROWS : (b + 1) * ROWS, :]
             by_cos = stage.tile([P, ROWS, D_ROPE], F32)
-            nc.vector.tensor_tensor(out=by_cos[:], in0=r_ps[:], in1=table[:, COS, :, :], op=ALU.mult)
+            nc.vector.tensor_tensor(out=by_cos[:], in0=r_ps, in1=table[:, COS, :, :], op=ALU.mult)
             by_sin = stage.tile([P, ROWS, D_ROPE], F32)
-            r_pairs = r_ps[:].rearrange("p j (m e) -> p (j m) e", e=2)
+            r_pairs = r_ps.rearrange("p j (m e) -> p (j m) e", e=2)
             sin_pairs = table[:, SIN, :, :].rearrange("p j (m e) -> p (j m) e", e=2)
             out_pairs = by_sin[:].rearrange("p j (m e) -> p (j m) e", e=2)
             for e in range(2):
@@ -225,56 +301,60 @@ def tile_multiheadlatentattention_pb_kernel(tc, x, Wkva, kv_a_norm_w, Wkvb, out_
                 )
             rotated = keep.tile([P, ROWS, D_ROPE], F32, name="rotated%d" % b)
             nc.vector.tensor_tensor(out=rotated[:], in0=by_cos[:], in1=by_sin[:], op=ALU.add)
-            rope_out[b] = rotated
+            return rotated
 
-        for g in range(GROUPS):
-            by_head = wb_raw[g][:].rearrange("p t (h f) -> p h f t", f=HEAD_COLS)
-            wv_grouped = stage.tile([P, V_COLS * PACK], BF16, align_bytes=64)
+        def spread(rotated, k_tile):
             nc.vector.tensor_copy(
-                out=wv_grouped[:].rearrange("p (h f t) -> p h f t", h=GROUP_HEADS, t=PACK),
-                in_=by_head[:, :, D_NOPE:HEAD_COLS, :],
+                out=k_tile[:, :, :, D_NOPE:],
+                in_=rotated[:].unsqueeze(1).to_broadcast([P, GROUP_HEADS, ROWS, D_ROPE]),
             )
-            wn_grouped = stage.tile([P, NOPE_COLS * PACK], BF16, align_bytes=64)
-            nc.scalar.copy(
-                out=wn_grouped[:].rearrange("p (h f t) -> p h f t", h=GROUP_HEADS, t=PACK),
-                in_=by_head[:, :, 0:D_NOPE, :],
-            )
-            quantise(wv_codes[:, g, :], wv_scales[:, g, :], wv_grouped[:])
-            quantise(wn_codes[:, g, :], wn_scales[:, g, :], wn_grouped[:])
 
+        rotated = {}
+        for g in range(GROUPS):
+            slot = g % K_BUFFERS
             heads = slice(g * GROUP_HEADS, (g + 1) * GROUP_HEADS)
+            if g > 0:
+                wv_grouped = regroup_v(g)
+                wn_grouped = regroup_nope(g)
+                quantise(wv_codes[:, g, :], wv_scales[:, g, :], wv_grouped[:])
+                quantise(wn_codes[:, g, :], wn_scales[:, g, :], wn_grouped[:])
+            v_ps = {}
+            nope_ps = {}
             for b in range(BATCH):
-                v_tile = outp.tile([P, GROUP_HEADS, ROWS, D_V], F32)
-                k_tile = outp.tile([P, GROUP_HEADS, ROWS, D_NOPE + D_ROPE], F32)
-                nope_ps = psum.tile([P, ROWS, NOPE_COLS], F32, tag="bank")
+                nope_ps[b] = psum.tile([P, ROWS, NOPE_COLS], F32, tag="bank", name="nope_ps%d" % b)
                 for j in range(ROWS):
-                    toks = slice(j * P, (j + 1) * P)
-                    v_ps = psum.tile([P, V_COLS], F32, tag="bank")
-                    for out_ap, codes, scales in (
-                        (v_ps[:], wv_codes, wv_scales),
-                        (nope_ps[:, j, :], wn_codes, wn_scales),
-                    ):
-                        nc.tensor.matmul_mx(
-                            out=out_ap,
-                            lhsT=h_codes[:, b, toks].bitcast(FP8X4),
-                            lhsT_scale=h_scales[:, b, toks],
-                            rhs=codes[:, g, :].bitcast(FP8X4),
-                            rhs_scale=scales[:, g, :],
-                            start=True,
-                            stop=True,
-                        )
-                    nc.scalar.copy(out=v_tile[:, :, j, :], in_=v_ps[:].rearrange("p (h f) -> p h f", h=GROUP_HEADS))
+                    toks = slice((b * ROWS + j) * P, (b * ROWS + j + 1) * P)
+                    v_ps[(b, j)] = psum.tile([P, V_COLS], F32, tag="bank", name="v_ps%d%d" % (b, j))
+                    mx_pass(
+                        v_ps[(b, j)][:], h_codes[:, toks], h_scales[:, toks],
+                        wv_codes[:, g, :], wv_scales[:, g, :], start=True, stop=True,
+                    )
+                for j in range(ROWS):
+                    toks = slice((b * ROWS + j) * P, (b * ROWS + j + 1) * P)
+                    mx_pass(
+                        nope_ps[b][:, j, :], h_codes[:, toks], h_scales[:, toks],
+                        wn_codes[:, g, :], wn_scales[:, g, :], start=True, stop=True,
+                    )
+            for b in range(BATCH):
+                v_tile = per_tile.tile([P, GROUP_HEADS, ROWS, D_V], F32)
+                for j in range(ROWS):
+                    nc.scalar.copy(
+                        out=v_tile[:, :, j, :], in_=v_ps[(b, j)][:].rearrange("p (h f) -> p h f", h=GROUP_HEADS)
+                    )
                 nc.sync.dma_start(
                     out=out_1[b, heads].rearrange("h (p j) f -> p h (j f)", j=ROWS),
                     in_=v_tile[:].rearrange("p h j f -> p h (j f)"),
                 )
-                nc.vector.tensor_copy(
+            for b in range(BATCH):
+                if g == 0:
+                    rotated[b] = rotate(b)
+                if g < K_BUFFERS:
+                    spread(rotated[b], k_tiles[(slot, b)])
+            for b in range(BATCH):
+                k_tile = k_tiles[(slot, b)]
+                nc.scalar.copy(
                     out=k_tile[:, :, :, 0:D_NOPE],
-                    in_=nope_ps[:].rearrange("p j (h f) -> p h j f", h=GROUP_HEADS),
-                )
-                nc.vector.tensor_copy(
-                    out=k_tile[:, :, :, D_NOPE:],
-                    in_=rope_out[b][:].unsqueeze(1).to_broadcast([P, GROUP_HEADS, ROWS, D_ROPE]),
+                    in_=nope_ps[b][:].rearrange("p j (h f) -> p h j f", h=GROUP_HEADS),
                 )
                 nc.sync.dma_start(
                     out=out_0[b, heads].rearrange("h (p j) f -> p h (j f)", j=ROWS),

@@ -33,7 +33,6 @@ GROUPS = HEADS // GROUP_HEADS
 GROUP_COLS = GROUP_HEADS * HEAD_COLS
 V_COLS = GROUP_HEADS * D_V
 NOPE_COLS = GROUP_HEADS * D_NOPE
-K_BUFFERS = 2
 RUN = 4
 
 ROUND_MAGIC = 1.5 * 2.0**23
@@ -68,14 +67,7 @@ def tile_multiheadlatentattention_pb_kernel(tc, x, Wkva, kv_a_norm_w, Wkvb, out_
             )
 
         gain_row = const.tile([P, LATENT], BF16)
-        nc.vector.memset(gain_row[:], 0.0)
-        nc.sync.dma_start(out=gain_row[0:1, :], in_=kv_a_norm_w.rearrange("(o n) -> o n", o=1))
-        x_raw = []
-        for b in range(BATCH):
-            for j in range(ROWS):
-                x_tile = raw.tile([P, D_MODEL], BF16, name="x_raw%d%d" % (b, j))
-                nc.sync.dma_start(out=x_tile[:], in_=x[b].rearrange("(p j) d -> p j d", j=ROWS)[:, j, :])
-                x_raw.append(x_tile)
+        nc.gpsimd.memset(gain_row[:], 0.0)
         wa_raw = []
         for c in range(A_PASSES):
             wa_tile = raw.tile([P, PACK, A_COLS], BF16, name="wa_raw%d" % c)
@@ -84,6 +76,14 @@ def tile_multiheadlatentattention_pb_kernel(tc, x, Wkva, kv_a_norm_w, Wkvb, out_
                 in_=Wkva[c * K_PASS : (c + 1) * K_PASS, :].rearrange("(u q e) n -> q u (e n)", u=2, e=2),
             )
             wa_raw.append(wa_tile)
+            if c == 0:
+                nc.sync.dma_start(out=gain_row[0:1, :], in_=kv_a_norm_w.rearrange("(o n) -> o n", o=1))
+        x_raw = []
+        for b in range(BATCH):
+            for j in range(ROWS):
+                x_tile = raw.tile([P, D_MODEL], BF16, name="x_raw%d%d" % (b, j))
+                nc.sync.dma_start(out=x_tile[:], in_=x[b].rearrange("(p j) d -> p j d", j=ROWS)[:, j, :])
+                x_raw.append(x_tile)
         wb_raw = []
         for g in range(GROUPS):
             wb_tile = raw.tile([P, PACK, GROUP_COLS], BF16, name="wb_raw%d" % g)
@@ -109,6 +109,10 @@ def tile_multiheadlatentattention_pb_kernel(tc, x, Wkva, kv_a_norm_w, Wkvb, out_
 
         ones = const.tile([P, P], BF16)
         nc.vector.memset(ones[:], 1.0)
+        gain_ps = psum.tile([P, LATENT], F32, tag="bank")
+        nc.tensor.matmul(out=gain_ps[:], lhsT=ones[:], rhs=gain_row[:], start=True, stop=True)
+        gain = const.tile([P, LATENT], F32)
+        nc.scalar.copy(out=gain[:], in_=gain_ps[:])
 
         per_pos = const.tile([P, D_ROPE], F32)
         nc.vector.memset(per_pos[:], 1.0)
@@ -151,6 +155,32 @@ def tile_multiheadlatentattention_pb_kernel(tc, x, Wkva, kv_a_norm_w, Wkvb, out_
         wn_codes = keep.tile([P, GROUPS, NOPE_COLS], U32, align_bytes=64)
         wn_scales = keep.tile([P, GROUPS, NOPE_COLS], U8, align_bytes=64)
 
+        HALF_COLS = A_COLS // 2
+
+        def regroup_wa(c):
+            grouped = stage.tile([P, A_COLS, PACK], BF16, align_bytes=64, name="wa_grouped%d" % c, tag="wa_grouped")
+            nc.vector.tensor_copy(
+                out=grouped[:, 0:HALF_COLS, :].rearrange("p (c i) t -> p c t i", i=RUN),
+                in_=wa_raw[c][:, :, 0:HALF_COLS].rearrange("p t (c i) -> p c t i", i=RUN),
+            )
+            nc.scalar.copy(
+                out=grouped[:, HALF_COLS:A_COLS, :].rearrange("p (c i) t -> p c t i", i=RUN),
+                in_=wa_raw[c][:, :, HALF_COLS:A_COLS].rearrange("p t (c i) -> p c t i", i=RUN),
+            )
+            return grouped
+
+        def quantise_wa(c, grouped):
+            for cols in (slice(0, LATENT), slice(LATENT, A_COLS)):
+                quantise(
+                    wa_codes[:, c, cols], wa_scales[:, c, cols], grouped[:, cols, :].rearrange("p n t -> p (n t)")
+                )
+
+        wa_grouped = [regroup_wa(0)]
+        for c in range(A_PASSES):
+            if c + 1 < A_PASSES:
+                wa_grouped.append(regroup_wa(c + 1))
+            quantise_wa(c, wa_grouped[c])
+
         for i in range(TILES):
             x_words = x_raw[i][:].bitcast(F32)
             x_grouped = per_tile.tile([P, A_PASSES * P * PACK], BF16, align_bytes=64)
@@ -167,45 +197,69 @@ def tile_multiheadlatentattention_pb_kernel(tc, x, Wkva, kv_a_norm_w, Wkvb, out_
                 )
             quantise(x_codes[:, i, :], x_scales[:, i, :], x_grouped[:])
 
-        gain_ps = psum.tile([P, LATENT], F32, tag="bank")
-        nc.tensor.matmul(out=gain_ps[:], lhsT=ones[:], rhs=gain_row[:], start=True, stop=True)
-        gain = const.tile([P, LATENT], F32)
-        nc.vector.tensor_copy(out=gain[:], in_=gain_ps[:])
+        nc.scalar.activation(out=table[:], in_=part[:], func=ACT.Sin, scale=2.0 * math.pi)
 
-        HALF_COLS = A_COLS // 2
-        latent_ps = []
-        for i in range(TILES):
-            latent_ps.append(psum.tile([P, LATENT], F32, tag="bank", name="latent_ps%d" % i))
-        wa_grouped = []
-        for c in range(A_PASSES):
-            grouped = per_tile.tile([P, A_COLS, PACK], BF16, align_bytes=64, name="wa_grouped%d" % c, tag="wa_grouped")
-            nc.vector.tensor_copy(
-                out=grouped[:, 0:HALF_COLS, :].rearrange("p (c i) t -> p c t i", i=RUN),
-                in_=wa_raw[c][:, :, 0:HALF_COLS].rearrange("p t (c i) -> p c t i", i=RUN),
-            )
-            nc.scalar.copy(
-                out=grouped[:, HALF_COLS:A_COLS, :].rearrange("p (c i) t -> p c t i", i=RUN),
-                in_=wa_raw[c][:, :, HALF_COLS:A_COLS].rearrange("p t (c i) -> p c t i", i=RUN),
-            )
-            wa_grouped.append(grouped)
-            quantise(
-                wa_codes[:, c, 0:LATENT], wa_scales[:, c, 0:LATENT],
-                grouped[:, 0:LATENT, :].rearrange("p n t -> p (n t)"),
-            )
-            toks = slice(c * P, (c + 1) * P)
-            for i in range(TILES):
+        latent_ps = {}
+        rope_ps = {}
+        hT_ps = {}
+        grouped_w = {}
+        rotated = {}
+        v_ps = {}
+        nope_ps = {}
+        mean_sq = const.tile([P, TILES], F32)
+        mean_eps = const.tile([P, TILES], F32)
+        rstd = const.tile([P, TILES], F32)
+        h_grouped = keep.tile([P, TILES, P, PACK], BF16, align_bytes=64)
+        k_tiles = []
+        for b in range(BATCH):
+            k_tiles.append(keep.tile([P, GROUP_HEADS, ROWS, D_NOPE + D_ROPE], F32, name="k_tile%d" % b))
+
+        def first_product(out, i, cols):
+            for c in range(A_PASSES):
+                toks = slice(c * P, (c + 1) * P)
                 mx_pass(
-                    latent_ps[i][:], x_codes[:, i, toks], x_scales[:, i, toks],
-                    wa_codes[:, c, 0:LATENT], wa_scales[:, c, 0:LATENT],
+                    out, x_codes[:, i, toks], x_scales[:, i, toks], wa_codes[:, c, cols], wa_scales[:, c, cols],
                     start=(c == 0), stop=(c == A_PASSES - 1),
                 )
 
-        nc.scalar.activation(out=table[:], in_=part[:], func=ACT.Sin, scale=2.0 * math.pi)
+        def latent_passes(i):
+            latent_ps[i] = psum.tile([P, LATENT], F32, tag="bank", name="latent_ps%d" % i)
+            first_product(latent_ps[i][:], i, slice(0, LATENT))
 
-        for c in range(A_PASSES):
+        def rope_passes(b):
+            rope_ps[b] = psum.tile([P, ROWS, D_ROPE], F32, tag="bank", name="rope_ps%d" % b)
+            for j in range(ROWS):
+                first_product(rope_ps[b][:, j, :], b * ROWS + j, slice(LATENT, A_COLS))
+
+        def sum_squares(i):
+            col = slice(i, i + 1)
+            squares = stage.tile([P, LATENT], BF16)
+            nc.scalar.activation(
+                out=squares[:], in_=latent_ps[i][:], func=ACT.Square, scale=1.0 / math.sqrt(LATENT),
+                accum_out=mean_sq[:, col],
+            )
+            nc.gpsimd.tensor_scalar(
+                out=mean_eps[:, col], in0=mean_sq[:, col], scalar1=1.0, scalar2=EPS, op0=ALU.mult, op1=ALU.add
+            )
+            nc.gpsimd.tensor_tensor(out=rstd[:, col], in0=mean_eps[:, col], in1=minus_half[:], op=ALU.pow)
+
+        def scale_and_transpose(i):
+            h = per_tile.tile([P, LATENT], BF16)
+            nc.vector.scalar_tensor_tensor(
+                out=h[:], in0=latent_ps[i][:], scalar=rstd[:, i : i + 1], in1=gain[:], op0=ALU.mult, op1=ALU.mult
+            )
+            hT_ps[i] = psum.tile([P, PACK, P], BF16, tag="bank", name="hT_ps%d" % i)
+            for t in range(PACK):
+                nc.tensor.transpose(hT_ps[i][:, t, :], h[:, t * P : (t + 1) * P], ident_bf[:])
+
+        def copy_h(i):
+            nc.scalar.copy(out=h_grouped[:, i, :, :], in_=hT_ps[i][:].rearrange("p t r -> p r t"))
+
+        def quantise_h(b):
+            toks = slice(b * ROWS * P, (b + 1) * ROWS * P)
             quantise(
-                wa_codes[:, c, LATENT:A_COLS], wa_scales[:, c, LATENT:A_COLS],
-                wa_grouped[c][:, LATENT:A_COLS, :].rearrange("p n t -> p (n t)"),
+                h_codes[:, toks], h_scales[:, toks],
+                h_grouped[:, b * ROWS : (b + 1) * ROWS, :, :].rearrange("p i r t -> p (i r t)"),
             )
 
         def regroup_wb(g, first_col, cols_per_head, grouped):
@@ -220,75 +274,21 @@ def tile_multiheadlatentattention_pb_kernel(tc, x, Wkva, kv_a_norm_w, Wkvb, out_
         def regroup_v(g):
             wv_grouped = stage.tile([P, V_COLS * PACK], BF16, align_bytes=64)
             regroup_wb(g, D_NOPE, D_V, wv_grouped)
-            return wv_grouped
+            grouped_w[("v", g)] = wv_grouped
 
         def regroup_nope(g):
             wn_grouped = stage.tile([P, NOPE_COLS * PACK], BF16, align_bytes=64)
             regroup_wb(g, 0, D_NOPE, wn_grouped)
-            return wn_grouped
+            grouped_w[("nope", g)] = wn_grouped
 
-        wv_grouped0 = regroup_v(0)
-        quantise(wv_codes[:, 0, :], wv_scales[:, 0, :], wv_grouped0[:])
+        def quantise_v(g):
+            quantise(wv_codes[:, g, :], wv_scales[:, g, :], grouped_w[("v", g)][:])
 
-        rope_ps = psum.tile([P, TILES, D_ROPE], F32, tag="bank")
-        for i in range(TILES):
-            for c in range(A_PASSES):
-                toks = slice(c * P, (c + 1) * P)
-                mx_pass(
-                    rope_ps[:, i, :], x_codes[:, i, toks], x_scales[:, i, toks],
-                    wa_codes[:, c, LATENT:A_COLS], wa_scales[:, c, LATENT:A_COLS],
-                    start=(c == 0), stop=(c == A_PASSES - 1),
-                )
-
-        mean_sq = const.tile([P, TILES], F32)
-        mean_eps = const.tile([P, TILES], F32)
-        rstd = const.tile([P, TILES], F32)
-        for i in range(TILES):
-            col = slice(i, i + 1)
-            squares = stage.tile([P, LATENT], BF16)
-            nc.scalar.activation(
-                out=squares[:], in_=latent_ps[i][:], func=ACT.Square, scale=1.0 / math.sqrt(LATENT),
-                accum_out=mean_sq[:, col],
-            )
-            nc.gpsimd.tensor_scalar(
-                out=mean_eps[:, col], in0=mean_sq[:, col], scalar1=1.0, scalar2=EPS, op0=ALU.mult, op1=ALU.add
-            )
-            nc.gpsimd.tensor_tensor(out=rstd[:, col], in0=mean_eps[:, col], in1=minus_half[:], op=ALU.pow)
-        hT = []
-        for i in range(TILES):
-            h = per_tile.tile([P, LATENT], BF16)
-            nc.vector.scalar_tensor_tensor(
-                out=h[:], in0=latent_ps[i][:], scalar=rstd[:, i : i + 1], in1=gain[:], op0=ALU.mult, op1=ALU.mult
-            )
-            hT_ps = psum.tile([P, PACK, P], BF16, tag="bank", name="hT_ps%d" % i)
-            for t in range(PACK):
-                nc.tensor.transpose(hT_ps[:, t, :], h[:, t * P : (t + 1) * P], ident_bf[:])
-            hT.append(hT_ps)
-        h_grouped = keep.tile([P, TILES, P, PACK], BF16, align_bytes=64)
-        for i in range(TILES):
-            nc.scalar.copy(out=h_grouped[:, i, :, :], in_=hT[i][:].rearrange("p t r -> p r t"))
-
-        def quantise_h(b):
-            toks = slice(b * ROWS * P, (b + 1) * ROWS * P)
-            quantise(
-                h_codes[:, toks], h_scales[:, toks],
-                h_grouped[:, b * ROWS : (b + 1) * ROWS, :, :].rearrange("p i r t -> p (i r t)"),
-            )
-
-        quantise_h(0)
-        wn_grouped0 = regroup_nope(0)
-        quantise_h(1)
-        quantise(wn_codes[:, 0, :], wn_scales[:, 0, :], wn_grouped0[:])
-
-        k_tiles = {}
-        for slot in range(K_BUFFERS):
-            for b in range(BATCH):
-                k_tiles[(slot, b)] = keep.tile(
-                    [P, GROUP_HEADS, ROWS, D_NOPE + D_ROPE], F32, name="k_tile%d%d" % (slot, b)
-                )
+        def quantise_nope(g):
+            quantise(wn_codes[:, g, :], wn_scales[:, g, :], grouped_w[("nope", g)][:])
 
         def rotate(b):
-            r_ps = rope_ps[:, b * ROWS : (b + 1) * ROWS, :]
+            r_ps = rope_ps[b][:]
             by_cos = stage.tile([P, ROWS, D_ROPE], F32)
             nc.vector.tensor_tensor(out=by_cos[:], in0=r_ps, in1=table[:, COS, :, :], op=ALU.mult)
             by_sin = stage.tile([P, ROWS, D_ROPE], F32)
@@ -299,64 +299,95 @@ def tile_multiheadlatentattention_pb_kernel(tc, x, Wkva, kv_a_norm_w, Wkvb, out_
                 nc.vector.tensor_tensor(
                     out=out_pairs[:, :, e], in0=r_pairs[:, :, 1 - e], in1=sin_pairs[:, :, e], op=ALU.mult
                 )
-            rotated = keep.tile([P, ROWS, D_ROPE], F32, name="rotated%d" % b)
-            nc.vector.tensor_tensor(out=rotated[:], in0=by_cos[:], in1=by_sin[:], op=ALU.add)
-            return rotated
+            rotated[b] = keep.tile([P, ROWS, D_ROPE], F32, name="rotated%d" % b)
+            nc.vector.tensor_tensor(out=rotated[b][:], in0=by_cos[:], in1=by_sin[:], op=ALU.add)
 
-        def spread(rotated, k_tile):
+        def spread(b):
             nc.vector.tensor_copy(
-                out=k_tile[:, :, :, D_NOPE:],
-                in_=rotated[:].unsqueeze(1).to_broadcast([P, GROUP_HEADS, ROWS, D_ROPE]),
+                out=k_tiles[b][:, :, :, D_NOPE:],
+                in_=rotated[b][:].unsqueeze(1).to_broadcast([P, GROUP_HEADS, ROWS, D_ROPE]),
             )
 
-        rotated = {}
-        for g in range(GROUPS):
-            slot = g % K_BUFFERS
+        def second_product(g, b):
+            nope_ps[(g, b)] = psum.tile([P, ROWS, NOPE_COLS], F32, tag="bank", name="nope_ps%d%d" % (g, b))
+            for j in range(ROWS):
+                toks = slice((b * ROWS + j) * P, (b * ROWS + j + 1) * P)
+                v_ps[(g, b, j)] = psum.tile([P, V_COLS], F32, tag="bank", name="v_ps%d%d%d" % (g, b, j))
+                mx_pass(
+                    v_ps[(g, b, j)][:], h_codes[:, toks], h_scales[:, toks],
+                    wv_codes[:, g, :], wv_scales[:, g, :], start=True, stop=True,
+                )
+            for j in range(ROWS):
+                toks = slice((b * ROWS + j) * P, (b * ROWS + j + 1) * P)
+                mx_pass(
+                    nope_ps[(g, b)][:, j, :], h_codes[:, toks], h_scales[:, toks],
+                    wn_codes[:, g, :], wn_scales[:, g, :], start=True, stop=True,
+                )
+
+        def store_v(g, b):
             heads = slice(g * GROUP_HEADS, (g + 1) * GROUP_HEADS)
-            if g > 0:
-                wv_grouped = regroup_v(g)
-                wn_grouped = regroup_nope(g)
-                quantise(wv_codes[:, g, :], wv_scales[:, g, :], wv_grouped[:])
-                quantise(wn_codes[:, g, :], wn_scales[:, g, :], wn_grouped[:])
-            v_ps = {}
-            nope_ps = {}
-            for b in range(BATCH):
-                nope_ps[b] = psum.tile([P, ROWS, NOPE_COLS], F32, tag="bank", name="nope_ps%d" % b)
-                for j in range(ROWS):
-                    toks = slice((b * ROWS + j) * P, (b * ROWS + j + 1) * P)
-                    v_ps[(b, j)] = psum.tile([P, V_COLS], F32, tag="bank", name="v_ps%d%d" % (b, j))
-                    mx_pass(
-                        v_ps[(b, j)][:], h_codes[:, toks], h_scales[:, toks],
-                        wv_codes[:, g, :], wv_scales[:, g, :], start=True, stop=True,
-                    )
-                for j in range(ROWS):
-                    toks = slice((b * ROWS + j) * P, (b * ROWS + j + 1) * P)
-                    mx_pass(
-                        nope_ps[b][:, j, :], h_codes[:, toks], h_scales[:, toks],
-                        wn_codes[:, g, :], wn_scales[:, g, :], start=True, stop=True,
-                    )
-            for b in range(BATCH):
-                v_tile = per_tile.tile([P, GROUP_HEADS, ROWS, D_V], F32)
-                for j in range(ROWS):
-                    nc.scalar.copy(
-                        out=v_tile[:, :, j, :], in_=v_ps[(b, j)][:].rearrange("p (h f) -> p h f", h=GROUP_HEADS)
-                    )
-                nc.sync.dma_start(
-                    out=out_1[b, heads].rearrange("h (p j) f -> p h (j f)", j=ROWS),
-                    in_=v_tile[:].rearrange("p h j f -> p h (j f)"),
-                )
-            for b in range(BATCH):
-                if g == 0:
-                    rotated[b] = rotate(b)
-                if g < K_BUFFERS:
-                    spread(rotated[b], k_tiles[(slot, b)])
-            for b in range(BATCH):
-                k_tile = k_tiles[(slot, b)]
+            v_tile = per_tile.tile([P, GROUP_HEADS, ROWS, D_V], F32)
+            for j in range(ROWS):
                 nc.scalar.copy(
-                    out=k_tile[:, :, :, 0:D_NOPE],
-                    in_=nope_ps[b][:].rearrange("p j (h f) -> p h j f", h=GROUP_HEADS),
+                    out=v_tile[:, :, j, :], in_=v_ps[(g, b, j)][:].rearrange("p (h f) -> p h f", h=GROUP_HEADS)
                 )
-                nc.sync.dma_start(
-                    out=out_0[b, heads].rearrange("h (p j) f -> p h (j f)", j=ROWS),
-                    in_=k_tile[:].rearrange("p h j f -> p h (j f)"),
-                )
+            nc.sync.dma_start(
+                out=out_1[b, heads].rearrange("h (p j) f -> p h (j f)", j=ROWS),
+                in_=v_tile[:].rearrange("p h j f -> p h (j f)"),
+            )
+
+        def store_k(g, b):
+            heads = slice(g * GROUP_HEADS, (g + 1) * GROUP_HEADS)
+            nc.scalar.copy(
+                out=k_tiles[b][:, :, :, 0:D_NOPE],
+                in_=nope_ps[(g, b)][:].rearrange("p j (h f) -> p h j f", h=GROUP_HEADS),
+            )
+            nc.sync.dma_start(
+                out=out_0[b, heads].rearrange("h (p j) f -> p h (j f)", j=ROWS),
+                in_=k_tiles[b][:].rearrange("p h j f -> p h (j f)"),
+            )
+
+        for i in range(TILES):
+            latent_passes(i)
+        regroup_v(0)
+        quantise_v(0)
+        for i in range(TILES):
+            sum_squares(i)
+        scale_and_transpose(0)
+        regroup_nope(0)
+        scale_and_transpose(1)
+        quantise_nope(0)
+        rope_passes(0)
+        scale_and_transpose(2)
+        scale_and_transpose(3)
+        for i in range(TILES):
+            copy_h(i)
+        quantise_h(0)
+        second_product(0, 0)
+        rotate(0)
+        spread(0)
+        rope_passes(1)
+        quantise_h(1)
+        store_v(0, 0)
+        store_k(0, 0)
+        regroup_v(1)
+        rotate(1)
+        second_product(0, 1)
+        quantise_v(1)
+        spread(1)
+        store_v(0, 1)
+        regroup_nope(1)
+        store_k(0, 1)
+        quantise_nope(1)
+        for g in range(1, GROUPS):
+            for b in range(BATCH):
+                second_product(g, b)
+            if g + 1 < GROUPS:
+                regroup_v(g + 1)
+                regroup_nope(g + 1)
+                quantise_v(g + 1)
+                quantise_nope(g + 1)
+            for b in range(BATCH):
+                store_v(g, b)
+            for b in range(BATCH):
+                store_k(g, b)

import math
from contextlib import ExitStack

import concourse.mybir as mybir
from concourse.masks import make_identity

F32 = mybir.dt.float32
BF16 = mybir.dt.bfloat16
I32 = mybir.dt.int32
U32 = mybir.dt.uint32
U8 = mybir.dt.uint8
FP8X4 = mybir.dt.float8_e4m3fn_x4
ALU = mybir.AluOpType
ACT = mybir.ActivationFunctionType

P = 128
PACK = 4
K_PASS = P * PACK

BATCH, SEQ, D_MODEL = 2, 256, 2048
HEADS, D_NOPE, D_ROPE, D_V = 16, 64, 128, 128
LATENT = 512
A_COLS = LATENT + D_ROPE
HEAD_COLS = D_NOPE + D_V
THETA = 10000.0
EPS = 1e-6

A_PASSES = D_MODEL // K_PASS
ROWS = SEQ // P
TILES = BATCH * ROWS
GROUP_HEADS = 4
GROUPS = HEADS // GROUP_HEADS
GROUP_COLS = GROUP_HEADS * HEAD_COLS
V_COLS = GROUP_HEADS * D_V
NOPE_COLS = GROUP_HEADS * D_NOPE
RUN = 4

ROUND_MAGIC = 1.5 * 2.0**23
COS, SIN = 0, 1

FLOPS = 2 * BATCH * SEQ * (D_MODEL * A_COLS + LATENT * HEADS * HEAD_COLS)


def tile_multiheadlatentattention_pb_kernel(tc, x, Wkva, kv_a_norm_w, Wkvb, out_0, out_1):
    nc = tc.nc
    with ExitStack() as ctx:
        const = ctx.enter_context(tc.tile_pool(name="const", bufs=1))
        raw = ctx.enter_context(tc.tile_pool(name="raw", bufs=1))
        keep = ctx.enter_context(tc.tile_pool(name="keep", bufs=1))
        stage = ctx.enter_context(tc.tile_pool(name="stage", bufs=2))
        per_tile = ctx.enter_context(tc.tile_pool(name="per_tile", bufs=TILES))
        psum = ctx.enter_context(tc.psum_pool(name="psum", bufs=8))
        ctx.enter_context(tc.manual_schedule())

        def quantise(codes, scales, grouped):
            nc.vector.quantize_mx(out=codes.bitcast(FP8X4), scales=scales, in_=grouped)

        def mx_pass(out, lhs_codes, lhs_scales, rhs_codes, rhs_scales, start, stop):
            nc.tensor.matmul_mx(
                out=out,
                lhsT=lhs_codes.bitcast(FP8X4),
                lhsT_scale=lhs_scales,
                rhs=rhs_codes.bitcast(FP8X4),
                rhs_scale=rhs_scales,
                start=start,
                stop=stop,
            )

        gain_row = const.tile([P, LATENT], BF16)
        nc.gpsimd.memset(gain_row[:], 0.0)
        wa_raw = []
        for c in range(A_PASSES):
            wa_tile = raw.tile([P, PACK, A_COLS], BF16, name="wa_raw%d" % c)
            nc.sync.dma_start(
                out=wa_tile[:].rearrange("q (u e) n -> q u (e n)", u=2),
                in_=Wkva[c * K_PASS : (c + 1) * K_PASS, :].rearrange("(u q e) n -> q u (e n)", u=2, e=2),
            )
            wa_raw.append(wa_tile)
            if c == 0:
                nc.sync.dma_start(out=gain_row[0:1, :], in_=kv_a_norm_w.rearrange("(o n) -> o n", o=1))
        x_raw = []
        for b in range(BATCH):
            for j in range(ROWS):
                x_tile = raw.tile([P, D_MODEL], BF16, name="x_raw%d%d" % (b, j))
                nc.sync.dma_start(out=x_tile[:], in_=x[b].rearrange("(p j) d -> p j d", j=ROWS)[:, j, :])
                x_raw.append(x_tile)
        wb_raw = []
        for g in range(GROUPS):
            wb_tile = raw.tile([P, PACK, GROUP_COLS], BF16, name="wb_raw%d" % g)
            nc.sync.dma_start(
                out=wb_tile[:],
                in_=Wkvb[:, g * GROUP_COLS : (g + 1) * GROUP_COLS].rearrange("(t p) n -> p t n", p=P),
            )
            wb_raw.append(wb_tile)

        ident_f32 = const.tile([P, P], F32)
        make_identity(nc, ident_f32[:])
        ident_bf = const.tile([P, P], BF16)
        make_identity(nc, ident_bf[:])
        pos_int = const.tile([P, ROWS], I32)
        nc.gpsimd.iota(pos_int[:], pattern=[[1, ROWS]], base=0, channel_multiplier=ROWS)
        minus_half = const.tile([P, 1], F32)
        nc.gpsimd.memset(minus_half[:], -0.5)
        zero_col = const.tile([P, 1], F32)
        nc.gpsimd.memset(zero_col[:], 0.0)

        warm = const.tile([P, 1], F32)
        nc.scalar.activation(out=warm[:], in_=zero_col[:], func=ACT.Sin)

        ones = const.tile([P, P], BF16)
        nc.vector.memset(ones[:], 1.0)
        gain_ps = psum.tile([P, LATENT], F32, tag="bank")
        nc.tensor.matmul(out=gain_ps[:], lhsT=ones[:], rhs=gain_row[:], start=True, stop=True)
        gain = const.tile([P, LATENT], F32)
        nc.scalar.copy(out=gain[:], in_=gain_ps[:])

        per_pos = const.tile([P, D_ROPE], F32)
        nc.vector.memset(per_pos[:], 1.0)
        for level in range(6):
            bit = 2**level
            has_bit = per_pos[:].rearrange("p (a two c) -> p a two c", two=2, c=bit)[:, :, 1, :]
            nc.vector.tensor_scalar_mul(out=has_bit, in0=has_bit, scalar1=THETA ** (-bit / 64.0))
        pos = const.tile([P, ROWS], F32)
        nc.vector.tensor_copy(out=pos[:], in_=pos_int[:])
        pos_turns = const.tile([P, ROWS], F32)
        nc.vector.tensor_scalar_mul(out=pos_turns[:], in0=pos[:], scalar1=1.0 / (2.0 * math.pi))
        turns = const.tile([P, 2, ROWS, D_ROPE], F32)
        for j in range(ROWS):
            nc.vector.tensor_scalar(
                out=turns[:, COS, j, :], in0=per_pos[:], scalar1=pos_turns[:, j : j + 1], scalar2=0.25,
                op0=ALU.mult, op1=ALU.add,
            )
            nc.vector.tensor_scalar(
                out=turns[:, SIN, j, :], in0=per_pos[:], scalar1=pos_turns[:, j : j + 1], scalar2=None,
                op0=ALU.mult,
            )
        whole = const.tile([P, 2, ROWS, D_ROPE], F32)
        nc.vector.tensor_scalar(
            out=whole[:], in0=turns[:], scalar1=ROUND_MAGIC, scalar2=ROUND_MAGIC, op0=ALU.add, op1=ALU.subtract
        )
        part = const.tile([P, 2, ROWS, D_ROPE], F32)
        nc.vector.tensor_tensor(out=part[:], in0=turns[:], in1=whole[:], op=ALU.subtract)
        sin_even = part[:, SIN, :, :].rearrange("p j (m e) -> p (j m) e", e=2)[:, :, 0]
        nc.vector.tensor_scalar_mul(out=sin_even, in0=sin_even, scalar1=-1.0)
        table = const.tile([P, 2, ROWS, D_ROPE], F32)

        x_codes = keep.tile([P, TILES, A_PASSES * P], U32, align_bytes=64)
        x_scales = keep.tile([P, TILES, A_PASSES * P], U8, align_bytes=64)
        wa_codes = keep.tile([P, A_PASSES, A_COLS], U32, align_bytes=64)
        wa_scales = keep.tile([P, A_PASSES, A_COLS], U8, align_bytes=64)
        h_codes = keep.tile([P, TILES * P], U32, align_bytes=64)
        h_scales = keep.tile([P, TILES * P], U8, align_bytes=64)
        wv_codes = keep.tile([P, GROUPS, V_COLS], U32, align_bytes=64)
        wv_scales = keep.tile([P, GROUPS, V_COLS], U8, align_bytes=64)
        wn_codes = keep.tile([P, GROUPS, NOPE_COLS], U32, align_bytes=64)
        wn_scales = keep.tile([P, GROUPS, NOPE_COLS], U8, align_bytes=64)

        HALF_COLS = A_COLS // 2

        def regroup_wa(c):
            grouped = stage.tile([P, A_COLS, PACK], BF16, align_bytes=64, name="wa_grouped%d" % c, tag="wa_grouped")
            nc.vector.tensor_copy(
                out=grouped[:, 0:HALF_COLS, :].rearrange("p (c i) t -> p c t i", i=RUN),
                in_=wa_raw[c][:, :, 0:HALF_COLS].rearrange("p t (c i) -> p c t i", i=RUN),
            )
            nc.scalar.copy(
                out=grouped[:, HALF_COLS:A_COLS, :].rearrange("p (c i) t -> p c t i", i=RUN),
                in_=wa_raw[c][:, :, HALF_COLS:A_COLS].rearrange("p t (c i) -> p c t i", i=RUN),
            )
            return grouped

        def quantise_wa(c, grouped):
            for cols in (slice(0, LATENT), slice(LATENT, A_COLS)):
                quantise(
                    wa_codes[:, c, cols], wa_scales[:, c, cols], grouped[:, cols, :].rearrange("p n t -> p (n t)")
                )

        wa_grouped = [regroup_wa(0)]
        for c in range(A_PASSES):
            if c + 1 < A_PASSES:
                wa_grouped.append(regroup_wa(c + 1))
            quantise_wa(c, wa_grouped[c])

        for i in range(TILES):
            x_words = x_raw[i][:].bitcast(F32)
            x_grouped = per_tile.tile([P, A_PASSES * P * PACK], BF16, align_bytes=64)
            xg_words = x_grouped[:].bitcast(F32).rearrange("p (c r u) -> p c r u", c=A_PASSES, u=2)
            for half in range(2):
                xT = psum.tile([P, 2, 2, P], F32, tag="bank")
                for c2 in range(2):
                    for u in range(2):
                        w0 = ((2 * half + c2) * 2 + u) * P
                        nc.tensor.transpose(xT[:, c2, u, :], x_words[:, w0 : w0 + P], ident_f32[:])
                nc.scalar.copy(
                    out=xg_words[:, 2 * half : 2 * half + 2, :, :],
                    in_=xT[:].rearrange("p c u r -> p c r u"),
                )
            quantise(x_codes[:, i, :], x_scales[:, i, :], x_grouped[:])

        nc.scalar.activation(out=table[:], in_=part[:], func=ACT.Sin, scale=2.0 * math.pi)

        latent_ps = {}
        rope_ps = {}
        hT_ps = {}
        grouped_w = {}
        rotated = {}
        v_ps = {}
        nope_ps = {}
        mean_sq = const.tile([P, TILES], F32)
        mean_eps = const.tile([P, TILES], F32)
        rstd = const.tile([P, TILES], F32)
        h_grouped = keep.tile([P, TILES, P, PACK], BF16, align_bytes=64)
        k_tiles = []
        for b in range(BATCH):
            k_tiles.append(keep.tile([P, GROUP_HEADS, ROWS, D_NOPE + D_ROPE], F32, name="k_tile%d" % b))

        def first_product(out, i, cols):
            for c in range(A_PASSES):
                toks = slice(c * P, (c + 1) * P)
                mx_pass(
                    out, x_codes[:, i, toks], x_scales[:, i, toks], wa_codes[:, c, cols], wa_scales[:, c, cols],
                    start=(c == 0), stop=(c == A_PASSES - 1),
                )

        def latent_passes(i):
            latent_ps[i] = psum.tile([P, LATENT], F32, tag="bank", name="latent_ps%d" % i)
            first_product(latent_ps[i][:], i, slice(0, LATENT))

        def rope_passes(b):
            rope_ps[b] = psum.tile([P, ROWS, D_ROPE], F32, tag="bank", name="rope_ps%d" % b)
            for j in range(ROWS):
                first_product(rope_ps[b][:, j, :], b * ROWS + j, slice(LATENT, A_COLS))

        def sum_squares(i):
            col = slice(i, i + 1)
            squares = stage.tile([P, LATENT], BF16)
            nc.scalar.activation(
                out=squares[:], in_=latent_ps[i][:], func=ACT.Square, scale=1.0 / math.sqrt(LATENT),
                accum_out=mean_sq[:, col],
            )
            nc.gpsimd.tensor_scalar(
                out=mean_eps[:, col], in0=mean_sq[:, col], scalar1=1.0, scalar2=EPS, op0=ALU.mult, op1=ALU.add
            )
            nc.gpsimd.tensor_tensor(out=rstd[:, col], in0=mean_eps[:, col], in1=minus_half[:], op=ALU.pow)

        def scale_and_transpose(i):
            h = per_tile.tile([P, LATENT], BF16)
            nc.vector.scalar_tensor_tensor(
                out=h[:], in0=latent_ps[i][:], scalar=rstd[:, i : i + 1], in1=gain[:], op0=ALU.mult, op1=ALU.mult
            )
            hT_ps[i] = psum.tile([P, PACK, P], BF16, tag="bank", name="hT_ps%d" % i)
            for t in range(PACK):
                nc.tensor.transpose(hT_ps[i][:, t, :], h[:, t * P : (t + 1) * P], ident_bf[:])

        def copy_h(i):
            nc.scalar.copy(out=h_grouped[:, i, :, :], in_=hT_ps[i][:].rearrange("p t r -> p r t"))

        def quantise_h(b):
            toks = slice(b * ROWS * P, (b + 1) * ROWS * P)
            quantise(
                h_codes[:, toks], h_scales[:, toks],
                h_grouped[:, b * ROWS : (b + 1) * ROWS, :, :].rearrange("p i r t -> p (i r t)"),
            )

        def regroup_wb(g, first_col, cols_per_head, grouped):
            by_head = wb_raw[g][:].rearrange("p t (h f) -> p h t f", f=HEAD_COLS)
            nc.vector.tensor_copy(
                out=grouped[:].rearrange("p (h c i t) -> p h c t i", h=GROUP_HEADS, i=RUN, t=PACK),
                in_=by_head[:, :, :, first_col : first_col + cols_per_head].rearrange(
                    "p h t (c i) -> p h c t i", i=RUN
                ),
            )

        def regroup_v(g):
            wv_grouped = stage.tile([P, V_COLS * PACK], BF16, align_bytes=64)
            regroup_wb(g, D_NOPE, D_V, wv_grouped)
            grouped_w[("v", g)] = wv_grouped

        def regroup_nope(g):
            wn_grouped = stage.tile([P, NOPE_COLS * PACK], BF16, align_bytes=64)
            regroup_wb(g, 0, D_NOPE, wn_grouped)
            grouped_w[("nope", g)] = wn_grouped

        def quantise_v(g):
            quantise(wv_codes[:, g, :], wv_scales[:, g, :], grouped_w[("v", g)][:])

        def quantise_nope(g):
            quantise(wn_codes[:, g, :], wn_scales[:, g, :], grouped_w[("nope", g)][:])

        def rotate(b):
            r_ps = rope_ps[b][:]
            by_cos = stage.tile([P, ROWS, D_ROPE], F32)
            nc.vector.tensor_tensor(out=by_cos[:], in0=r_ps, in1=table[:, COS, :, :], op=ALU.mult)
            by_sin = stage.tile([P, ROWS, D_ROPE], F32)
            r_pairs = r_ps.rearrange("p j (m e) -> p (j m) e", e=2)
            sin_pairs = table[:, SIN, :, :].rearrange("p j (m e) -> p (j m) e", e=2)
            out_pairs = by_sin[:].rearrange("p j (m e) -> p (j m) e", e=2)
            for e in range(2):
                nc.vector.tensor_tensor(
                    out=out_pairs[:, :, e], in0=r_pairs[:, :, 1 - e], in1=sin_pairs[:, :, e], op=ALU.mult
                )
            rotated[b] = keep.tile([P, ROWS, D_ROPE], F32, name="rotated%d" % b)
            nc.vector.tensor_tensor(out=rotated[b][:], in0=by_cos[:], in1=by_sin[:], op=ALU.add)

        def spread(b):
            nc.vector.tensor_copy(
                out=k_tiles[b][:, :, :, D_NOPE:],
                in_=rotated[b][:].unsqueeze(1).to_broadcast([P, GROUP_HEADS, ROWS, D_ROPE]),
            )

        def second_product(g, b):
            nope_ps[(g, b)] = psum.tile([P, ROWS, NOPE_COLS], F32, tag="bank", name="nope_ps%d%d" % (g, b))
            for j in range(ROWS):
                toks = slice((b * ROWS + j) * P, (b * ROWS + j + 1) * P)
                v_ps[(g, b, j)] = psum.tile([P, V_COLS], F32, tag="bank", name="v_ps%d%d%d" % (g, b, j))
                mx_pass(
                    v_ps[(g, b, j)][:], h_codes[:, toks], h_scales[:, toks],
                    wv_codes[:, g, :], wv_scales[:, g, :], start=True, stop=True,
                )
            for j in range(ROWS):
                toks = slice((b * ROWS + j) * P, (b * ROWS + j + 1) * P)
                mx_pass(
                    nope_ps[(g, b)][:, j, :], h_codes[:, toks], h_scales[:, toks],
                    wn_codes[:, g, :], wn_scales[:, g, :], start=True, stop=True,
                )

        def store_v(g, b):
            heads = slice(g * GROUP_HEADS, (g + 1) * GROUP_HEADS)
            v_tile = per_tile.tile([P, GROUP_HEADS, ROWS, D_V], F32)
            for j in range(ROWS):
                nc.scalar.copy(
                    out=v_tile[:, :, j, :], in_=v_ps[(g, b, j)][:].rearrange("p (h f) -> p h f", h=GROUP_HEADS)
                )
            nc.sync.dma_start(
                out=out_1[b, heads].rearrange("h (p j) f -> p h (j f)", j=ROWS),
                in_=v_tile[:].rearrange("p h j f -> p h (j f)"),
            )

        def store_k(g, b):
            heads = slice(g * GROUP_HEADS, (g + 1) * GROUP_HEADS)
            nc.scalar.copy(
                out=k_tiles[b][:, :, :, 0:D_NOPE],
                in_=nope_ps[(g, b)][:].rearrange("p j (h f) -> p h j f", h=GROUP_HEADS),
            )
            nc.sync.dma_start(
                out=out_0[b, heads].rearrange("h (p j) f -> p h (j f)", j=ROWS),
                in_=k_tiles[b][:].rearrange("p h j f -> p h (j f)"),
            )

        for i in range(TILES):
            latent_passes(i)
        regroup_v(0)
        quantise_v(0)
        for i in range(TILES):
            sum_squares(i)
        scale_and_transpose(0)
        regroup_nope(0)
        scale_and_transpose(1)
        quantise_nope(0)
        rope_passes(0)
        scale_and_transpose(2)
        scale_and_transpose(3)
        for i in range(TILES):
            copy_h(i)
        quantise_h(0)
        second_product(0, 0)
        rotate(0)
        spread(0)
        rope_passes(1)
        quantise_h(1)
        store_v(0, 0)
        store_k(0, 0)
        regroup_v(1)
        rotate(1)
        second_product(0, 1)
        quantise_v(1)
        spread(1)
        store_v(0, 1)
        regroup_nope(1)
        store_k(0, 1)
        quantise_nope(1)
        for g in range(1, GROUPS):
            for b in range(BATCH):
                second_product(g, b)
            if g + 1 < GROUPS:
                regroup_v(g + 1)
                regroup_nope(g + 1)
                quantise_v(g + 1)
                quantise_nope(g + 1)
            for b in range(BATCH):
                store_v(g, b)
            for b in range(BATCH):
                store_k(g, b)
